import numpy as np
import ml_dtypes

BF16 = ml_dtypes.bfloat16


def bf(x):
    return np.asarray(x, np.float32).astype(BF16)


def f32(x):
    return np.asarray(x, np.float32)


def f64(x):
    return np.asarray(x).astype(np.float64)


def striped(idx):
    return np.tile(idx.reshape(-1, 16).T, (8, 1))


M0, M1, M2, D1, D2, C, FAN, SC, HID, S, N = 32, 64, 32, 3, 5, 384, 6144, 256, 128, 1024, 2048
ALPHA = 1.0 / np.sqrt(FAN)


def silu(t):
    return t / (1.0 + np.exp(-t))


def split(a):
    s = a[:M0]
    v = a[M0:M0 + D1 * M1].reshape(D1, M1, -1)
    t = a[M0 + D1 * M1:].reshape(D2, M2, -1)
    return s, v, t


def setup_inputs():
    return {"x": f32(np.random.standard_normal((C, S))), "x_dst": f32(np.random.standard_normal((C, N))), "w0": bf(np.random.standard_normal((M0 * M0, SC))), "w1": bf(np.random.standard_normal((M1 * M1, SC))), "w2": bf(np.random.standard_normal((M2 * M2, SC))), "a1": bf(np.random.standard_normal((SC, HID)) / np.sqrt(SC)), "b1": f32(0.1 * np.random.standard_normal((HID, 1))), "offs": striped(np.random.permutation(np.tile(np.arange(S), 2))[:N])}


def reference(x, x_dst, w0, w1, w2, a1, b1, offs):
    idx = offs[:16].T.reshape(-1)
    s1, v1, t1 = split(f64(x)[:, idx])
    s2, v2, t2 = split(f64(x_dst))
    z0 = (s1[:, None, :] * s2[None, :, :]).reshape(M0 * M0, -1)
    z1 = np.einsum('muj,mvj->uvj', v1, v2).reshape(M1 * M1, -1)
    z2 = np.einsum('muj,mvj->uvj', t1, t2).reshape(M2 * M2, -1)
    e = ALPHA * (f64(w0).T @ z0 + (f64(w1).T @ z1) / np.sqrt(D1) + (f64(w2).T @ z2) / np.sqrt(D2))
    return silu(f64(a1).T @ e + f64(b1))

@@ -1,0 +1,136 @@
+import math
+
+import concourse.mybir as mybir
+
+F32 = mybir.dt.float32
+BF16 = mybir.dt.bfloat16
+U16 = mybir.dt.uint16
+MULT = mybir.AluOpType.mult
+COPY = mybir.ActivationFunctionType.Copy
+SILU = mybir.ActivationFunctionType.Silu
+
+P = 128
+S = 1024
+N = 2048
+FAN = 6144
+SC = 256
+HID = 128
+U_PER = 8
+V_PER = 16
+PIECE = S
+BANK = 512
+PIECES = N // PIECE
+BANKS_PER_PIECE = PIECE // BANK
+E_BLOCKS = SC // P
+
+FLOPS = 2 * N * (FAN * SC + SC * HID)
+
+
+def tile_edgedecoder_b_kernel(tc, x, x_dst, w0, w1, w2, a1, b1, offs, out):
+    nc = tc.nc
+    alpha = 1.0 / math.sqrt(FAN)
+    kinds = (
+        (0, 32, 1, w0, alpha),
+        (32, 64, 3, w1, alpha / math.sqrt(3.0)),
+        (224, 32, 5, w2, alpha / math.sqrt(5.0)),
+    )
+    product_tiles = sum(
+        comps * (mult // U_PER) * (mult // V_PER) for row0, mult, comps, w, factor in kinds
+    )
+
+    with (
+        tc.tile_pool(name="held", bufs=1) as held,
+        tc.tile_pool(name="windows", bufs=16) as windows,
+        tc.tile_pool(name="others", bufs=3) as others,
+        tc.tile_pool(name="products", bufs=3) as products,
+        tc.tile_pool(name="rounded", bufs=3) as rounded,
+        tc.tile_pool(name="tail", bufs=2) as tail,
+        tc.psum_pool(name="psum", bufs=1) as psum,
+    ):
+        offsets = held.tile([P, N // 16], U16, name="offsets")
+        nc.sync.dma_start(offsets[:], offs)
+
+        a1_sb = held.tile([P, E_BLOCKS, HID], BF16, name="a1_sb")
+        nc.scalar.dma_start(a1_sb[:], a1.rearrange("(blk p) r -> p blk r", p=P))
+        b1_sb = held.tile([P, 1], F32, name="b1_sb")
+        nc.scalar.dma_start(b1_sb[:], b1)
+
+        e_ps = [
+            [psum.tile([P, BANK], F32, name="e_ps%d_%d" % (blk, bank)) for bank in range(N // BANK)]
+            for blk in range(E_BLOCKS)
+        ]
+
+        done = 0
+        for kind, (row0, mult, comps, w, factor) in enumerate(kinds):
+            u_groups = mult // U_PER
+            v_groups = mult // V_PER
+            w_vu = w.rearrange("(u v) k -> v u k", v=mult)
+            w_sb = held.tile([P, v_groups * u_groups, SC], BF16, name="w_sb%d" % kind)
+            for m in range(comps):
+                base = row0 + mult * m
+                wins = []
+                for vg in range(v_groups):
+                    v_lo = V_PER * vg
+                    other = others.tile([P, N], F32, name="other")
+                    nc.sync.dma_start(
+                        other[:],
+                        x_dst[base + v_lo : base + v_lo + V_PER, :]
+                        .unsqueeze(1)
+                        .to_broadcast([V_PER, U_PER, N]),
+                    )
+                    for ug in range(u_groups):
+                        u_lo = U_PER * ug
+                        pair_block = vg * u_groups + ug
+                        if vg == 0:
+                            win = windows.tile([P, S], F32, name="win")
+                            nc.sync.dma_start(
+                                win[:],
+                                x[base + u_lo : base + u_lo + U_PER, :]
+                                .unsqueeze(0)
+                                .to_broadcast([V_PER, U_PER, S]),
+                            )
+                            wins.append(win)
+                        if m == 0:
+                            nc.sync.dma_start(
+                                w_sb[:, pair_block, :],
+                                w_vu[v_lo : v_lo + V_PER, u_lo : u_lo + U_PER, :],
+                            )
+                        for piece in range(PIECES):
+                            prod = products.tile([P, PIECE], F32, name="prod")
+                            nc.vector.tensor_tensor(
+                                prod[:],
+                                wins[ug][:].indirect(
+                                    offsets[:, piece * (PIECE // 16) : (piece + 1) * (PIECE // 16)]
+                                ),
+                                other[:, piece * PIECE : (piece + 1) * PIECE],
+                                MULT,
+                            )
+                            z_bf = rounded.tile([P, PIECE], BF16, name="z_bf")
+                            nc.scalar.activation(z_bf[:], prod[:], COPY, scale=factor)
+                            for blk in range(E_BLOCKS):
+                                for sub in range(BANKS_PER_PIECE):
+                                    nc.tensor.matmul(
+                                        e_ps[blk][piece * BANKS_PER_PIECE + sub][:],
+                                        w_sb[:, pair_block, blk * P : (blk + 1) * P],
+                                        z_bf[:, sub * BANK : (sub + 1) * BANK],
+                                        start=(done == 0),
+                                        stop=(done == product_tiles - 1),
+                                    )
+                        done += 1
+
+        for bank in range(N // BANK):
+            e_bf = [tail.tile([P, BANK], BF16, name="e_bf%d" % blk) for blk in range(E_BLOCKS)]
+            nc.vector.tensor_copy(e_bf[0][:], e_ps[0][bank][:])
+            nc.scalar.copy(e_bf[1][:], e_ps[1][bank][:])
+            h_ps = psum.tile([P, BANK], F32, name="h_ps", tag="e_ps0_%d" % bank)
+            for blk in range(E_BLOCKS):
+                nc.tensor.matmul(
+                    h_ps[:],
+                    a1_sb[:, blk, :],
+                    e_bf[blk][:],
+                    start=(blk == 0),
+                    stop=(blk == E_BLOCKS - 1),
+                )
+            out_sb = tail.tile([P, BANK], F32, name="out_sb")
+            nc.scalar.activation(out_sb[:], h_ps[:], SILU, bias=b1_sb[:, 0:1])
+            nc.sync.dma_start(out[:, bank * BANK : (bank + 1) * BANK], out_sb[:])

@@ -41,7 +41,7 @@ def tile_edgedecoder_b_kernel(tc, x, x_dst, w0, w1, w2, a1, b1, offs, out):
     with (
         tc.tile_pool(name="held", bufs=1) as held,
         tc.tile_pool(name="windows", bufs=16) as windows,
-        tc.tile_pool(name="others", bufs=3) as others,
+        tc.tile_pool(name="others", bufs=6) as others,
         tc.tile_pool(name="products", bufs=3) as products,
         tc.tile_pool(name="rounded", bufs=3) as rounded,
         tc.tile_pool(name="tail", bufs=2) as tail,
@@ -54,13 +54,15 @@ def tile_edgedecoder_b_kernel(tc, x, x_dst, w0, w1, w2, a1, b1, offs, out):
         nc.scalar.dma_start(a1_sb[:], a1.rearrange("(blk p) r -> p blk r", p=P))
         b1_sb = held.tile([P, 1], F32, name="b1_sb")
         nc.scalar.dma_start(b1_sb[:], b1)
+        silu_first = held.tile([P, 1], F32, name="silu_first")
+        nc.scalar.activation(silu_first[:], b1_sb[:], SILU)
 
         e_ps = [
             [psum.tile([P, BANK], F32, name="e_ps%d_%d" % (blk, bank)) for bank in range(N // BANK)]
             for blk in range(E_BLOCKS)
         ]
 
-        done = 0
+        added = [0] * PIECES
         for kind, (row0, mult, comps, w, factor) in enumerate(kinds):
             u_groups = mult // U_PER
             v_groups = mult // V_PER
@@ -71,56 +73,59 @@ def tile_edgedecoder_b_kernel(tc, x, x_dst, w0, w1, w2, a1, b1, offs, out):
                 wins = []
                 for vg in range(v_groups):
                     v_lo = V_PER * vg
-                    other = others.tile([P, N], F32, name="other")
-                    nc.sync.dma_start(
-                        other[:],
-                        x_dst[base + v_lo : base + v_lo + V_PER, :]
-                        .unsqueeze(1)
-                        .to_broadcast([V_PER, U_PER, N]),
-                    )
-                    for ug in range(u_groups):
-                        u_lo = U_PER * ug
-                        pair_block = vg * u_groups + ug
-                        if vg == 0:
-                            win = windows.tile([P, S], F32, name="win")
-                            nc.sync.dma_start(
-                                win[:],
-                                x[base + u_lo : base + u_lo + U_PER, :]
-                                .unsqueeze(0)
-                                .to_broadcast([V_PER, U_PER, S]),
-                            )
-                            wins.append(win)
-                        if m == 0:
-                            nc.sync.dma_start(
-                                w_sb[:, pair_block, :],
-                                w_vu[v_lo : v_lo + V_PER, u_lo : u_lo + U_PER, :],
-                            )
-                        for piece in range(PIECES):
+                    for piece in range(PIECES):
+                        other = others.tile([P, PIECE], F32, name="other")
+                        nc.sync.dma_start(
+                            other[:],
+                            x_dst[base + v_lo : base + v_lo + V_PER, piece * PIECE : (piece + 1) * PIECE]
+                            .unsqueeze(1)
+                            .to_broadcast([V_PER, U_PER, PIECE]),
+                        )
+                        for ug in range(u_groups):
+                            u_lo = U_PER * ug
+                            pair_block = vg * u_groups + ug
+                            if vg == 0 and piece == 0:
+                                win = windows.tile([P, S], F32, name="win")
+                                nc.sync.dma_start(
+                                    win[:],
+                                    x[base + u_lo : base + u_lo + U_PER, :]
+                                    .unsqueeze(0)
+                                    .to_broadcast([V_PER, U_PER, S]),
+                                )
+                                wins.append(win)
+                            if m == 0 and piece == 0:
+                                nc.sync.dma_start(
+                                    w_sb[:, pair_block, :],
+                                    w_vu[v_lo : v_lo + V_PER, u_lo : u_lo + U_PER, :],
+                                )
                             prod = products.tile([P, PIECE], F32, name="prod")
                             nc.vector.tensor_tensor(
                                 prod[:],
                                 wins[ug][:].indirect(
                                     offsets[:, piece * (PIECE // 16) : (piece + 1) * (PIECE // 16)]
                                 ),
-                                other[:, piece * PIECE : (piece + 1) * PIECE],
+                                other[:],
                                 MULT,
                             )
                             z_bf = rounded.tile([P, PIECE], BF16, name="z_bf")
                             nc.scalar.activation(z_bf[:], prod[:], COPY, scale=factor)
-                            for blk in range(E_BLOCKS):
-                                for sub in range(BANKS_PER_PIECE):
+                            for sub in range(BANKS_PER_PIECE):
+                                for blk in range(E_BLOCKS):
                                     nc.tensor.matmul(
                                         e_ps[blk][piece * BANKS_PER_PIECE + sub][:],
                                         w_sb[:, pair_block, blk * P : (blk + 1) * P],
                                         z_bf[:, sub * BANK : (sub + 1) * BANK],
-                                        start=(done == 0),
-                                        stop=(done == product_tiles - 1),
+                                        start=(added[piece] == 0),
+                                        stop=(added[piece] == product_tiles - 1),
                                     )
-                        done += 1
+                            added[piece] += 1
 
         for bank in range(N // BANK):
             e_bf = [tail.tile([P, BANK], BF16, name="e_bf%d" % blk) for blk in range(E_BLOCKS)]
-            nc.vector.tensor_copy(e_bf[0][:], e_ps[0][bank][:])
+            if bank // BANKS_PER_PIECE == PIECES - 1:
+                nc.vector.tensor_copy(e_bf[0][:], e_ps[0][bank][:])
+            else:
+                nc.scalar.copy(e_bf[0][:], e_ps[0][bank][:])
             nc.scalar.copy(e_bf[1][:], e_ps[1][bank][:])
             h_ps = psum.tile([P, BANK], F32, name="h_ps", tag="e_ps0_%d" % bank)
             for blk in range(E_BLOCKS):

@@ -40,10 +40,10 @@ def tile_edgedecoder_b_kernel(tc, x, x_dst, w0, w1, w2, a1, b1, offs, out):
 
     with (
         tc.tile_pool(name="held", bufs=1) as held,
-        tc.tile_pool(name="windows", bufs=16) as windows,
-        tc.tile_pool(name="others", bufs=6) as others,
-        tc.tile_pool(name="products", bufs=3) as products,
-        tc.tile_pool(name="rounded", bufs=3) as rounded,
+        tc.tile_pool(name="windows", bufs=24) as windows,
+        tc.tile_pool(name="others", bufs=12) as others,
+        tc.tile_pool(name="products", bufs=4) as products,
+        tc.tile_pool(name="rounded", bufs=4) as rounded,
         tc.tile_pool(name="tail", bufs=2) as tail,
         tc.psum_pool(name="psum", bufs=1) as psum,
     ):

@@ -19,8 +19,8 @@ U_PER = 8
 V_PER = 16
 PIECE = S
 BANK = 512
-PIECES = N // PIECE
-BANKS_PER_PIECE = PIECE // BANK
+BANKS = N // BANK
+TOGETHER = 2
 E_BLOCKS = SC // P
 
 FLOPS = 2 * N * (FAN * SC + SC * HID)
@@ -40,8 +40,8 @@ def tile_edgedecoder_b_kernel(tc, x, x_dst, w0, w1, w2, a1, b1, offs, out):
 
     with (
         tc.tile_pool(name="held", bufs=1) as held,
-        tc.tile_pool(name="windows", bufs=24) as windows,
-        tc.tile_pool(name="others", bufs=12) as others,
+        tc.tile_pool(name="windows", bufs=4 * TOGETHER) as windows,
+        tc.tile_pool(name="others", bufs=16) as others,
         tc.tile_pool(name="products", bufs=4) as products,
         tc.tile_pool(name="rounded", bufs=4) as rounded,
         tc.tile_pool(name="tail", bufs=2) as tail,
@@ -58,11 +58,40 @@ def tile_edgedecoder_b_kernel(tc, x, x_dst, w0, w1, w2, a1, b1, offs, out):
         nc.scalar.activation(silu_first[:], b1_sb[:], SILU)
 
         e_ps = [
-            [psum.tile([P, BANK], F32, name="e_ps%d_%d" % (blk, bank)) for bank in range(N // BANK)]
+            [psum.tile([P, BANK], F32, name="e_ps%d_%d" % (blk, bank)) for bank in range(BANKS)]
             for blk in range(E_BLOCKS)
         ]
 
-        added = [0] * PIECES
+        e_bf = {}
+        h_ps = {}
+
+        def round_e(bank):
+            e_bf[bank] = [tail.tile([P, BANK], BF16, name="e_bf%d" % blk) for blk in range(E_BLOCKS)]
+            if bank == BANKS - 1:
+                nc.vector.tensor_copy(e_bf[bank][0][:], e_ps[0][bank][:])
+            else:
+                nc.scalar.copy(e_bf[bank][0][:], e_ps[0][bank][:])
+            nc.scalar.copy(e_bf[bank][1][:], e_ps[1][bank][:])
+
+        def multiply_by_a1(bank):
+            h_ps[bank] = psum.tile([P, BANK], F32, name="h_ps", tag="e_ps0_%d" % bank)
+            for blk in range(E_BLOCKS):
+                nc.tensor.matmul(
+                    h_ps[bank][:],
+                    a1_sb[:, blk, :],
+                    e_bf[bank][blk][:],
+                    start=(blk == 0),
+                    stop=(blk == E_BLOCKS - 1),
+                )
+
+        def silu_and_store(bank):
+            out_sb = tail.tile([P, BANK], F32, name="out_sb")
+            nc.scalar.activation(out_sb[:], h_ps[bank][:], SILU, bias=b1_sb[:, 0:1])
+            nc.sync.dma_start(out[:, bank * BANK : (bank + 1) * BANK], out_sb[:])
+
+        mlp_steps = (round_e, multiply_by_a1, silu_and_store)
+
+        added = [0] * BANKS
         for kind, (row0, mult, comps, w, factor) in enumerate(kinds):
             u_groups = mult // U_PER
             v_groups = mult // V_PER
@@ -70,72 +99,63 @@ def tile_edgedecoder_b_kernel(tc, x, x_dst, w0, w1, w2, a1, b1, offs, out):
             w_sb = held.tile([P, v_groups * u_groups, SC], BF16, name="w_sb%d" % kind)
             for m in range(comps):
                 base = row0 + mult * m
-                wins = []
-                for vg in range(v_groups):
-                    v_lo = V_PER * vg
-                    for piece in range(PIECES):
-                        other = others.tile([P, PIECE], F32, name="other")
-                        nc.sync.dma_start(
-                            other[:],
-                            x_dst[base + v_lo : base + v_lo + V_PER, piece * PIECE : (piece + 1) * PIECE]
-                            .unsqueeze(1)
-                            .to_broadcast([V_PER, U_PER, PIECE]),
-                        )
-                        for ug in range(u_groups):
-                            u_lo = U_PER * ug
-                            pair_block = vg * u_groups + ug
-                            if vg == 0 and piece == 0:
-                                win = windows.tile([P, S], F32, name="win")
+                dst = {}
+                for ug0 in range(0, u_groups, TOGETHER):
+                    wins = {}
+                    closing = kind == len(kinds) - 1 and m == comps - 1 and ug0 == u_groups - TOGETHER
+                    cols = BANK if closing else PIECE
+                    for part in range(N // cols):
+                        first = part * cols
+                        piece = first // PIECE
+                        for vg in range(v_groups):
+                            v_lo = V_PER * vg
+                            if ug0 == 0:
+                                dst[vg, piece] = others.tile([P, PIECE], F32, name="other")
                                 nc.sync.dma_start(
-                                    win[:],
-                                    x[base + u_lo : base + u_lo + U_PER, :]
-                                    .unsqueeze(0)
-                                    .to_broadcast([V_PER, U_PER, S]),
+                                    dst[vg, piece][:],
+                                    x_dst[base + v_lo : base + v_lo + V_PER, first : first + PIECE]
+                                    .unsqueeze(1)
+                                    .to_broadcast([V_PER, U_PER, PIECE]),
                                 )
-                                wins.append(win)
-                            if m == 0 and piece == 0:
-                                nc.sync.dma_start(
-                                    w_sb[:, pair_block, :],
-                                    w_vu[v_lo : v_lo + V_PER, u_lo : u_lo + U_PER, :],
-                                )
-                            prod = products.tile([P, PIECE], F32, name="prod")
-                            nc.vector.tensor_tensor(
-                                prod[:],
-                                wins[ug][:].indirect(
-                                    offsets[:, piece * (PIECE // 16) : (piece + 1) * (PIECE // 16)]
-                                ),
-                                other[:],
-                                MULT,
-                            )
-                            z_bf = rounded.tile([P, PIECE], BF16, name="z_bf")
-                            nc.scalar.activation(z_bf[:], prod[:], COPY, scale=factor)
-                            for sub in range(BANKS_PER_PIECE):
-                                for blk in range(E_BLOCKS):
-                                    nc.tensor.matmul(
-                                        e_ps[blk][piece * BANKS_PER_PIECE + sub][:],
-                                        w_sb[:, pair_block, blk * P : (blk + 1) * P],
-                                        z_bf[:, sub * BANK : (sub + 1) * BANK],
-                                        start=(added[piece] == 0),
-                                        stop=(added[piece] == product_tiles - 1),
+                            other = dst[vg, piece][:, first - piece * PIECE : first - piece * PIECE + cols]
+                            for ug in range(ug0, ug0 + TOGETHER):
+                                u_lo = U_PER * ug
+                                pair_block = vg * u_groups + ug
+                                if part == 0 and vg == 0:
+                                    wins[ug] = windows.tile([P, S], F32, name="win")
+                                    nc.sync.dma_start(
+                                        wins[ug][:],
+                                        x[base + u_lo : base + u_lo + U_PER, :]
+                                        .unsqueeze(0)
+                                        .to_broadcast([V_PER, U_PER, S]),
                                     )
-                            added[piece] += 1
-
-        for bank in range(N // BANK):
-            e_bf = [tail.tile([P, BANK], BF16, name="e_bf%d" % blk) for blk in range(E_BLOCKS)]
-            if bank // BANKS_PER_PIECE == PIECES - 1:
-                nc.vector.tensor_copy(e_bf[0][:], e_ps[0][bank][:])
-            else:
-                nc.scalar.copy(e_bf[0][:], e_ps[0][bank][:])
-            nc.scalar.copy(e_bf[1][:], e_ps[1][bank][:])
-            h_ps = psum.tile([P, BANK], F32, name="h_ps", tag="e_ps0_%d" % bank)
-            for blk in range(E_BLOCKS):
-                nc.tensor.matmul(
-                    h_ps[:],
-                    a1_sb[:, blk, :],
-                    e_bf[blk][:],
-                    start=(blk == 0),
-                    stop=(blk == E_BLOCKS - 1),
-                )
-            out_sb = tail.tile([P, BANK], F32, name="out_sb")
-            nc.scalar.activation(out_sb[:], h_ps[:], SILU, bias=b1_sb[:, 0:1])
-            nc.sync.dma_start(out[:, bank * BANK : (bank + 1) * BANK], out_sb[:])
+                                if m == 0 and part == 0:
+                                    nc.sync.dma_start(
+                                        w_sb[:, pair_block, :],
+                                        w_vu[v_lo : v_lo + V_PER, u_lo : u_lo + U_PER, :],
+                                    )
+                                prod = products.tile([P, cols], F32, name="prod")
+                                nc.vector.tensor_tensor(
+                                    prod[:],
+                                    wins[ug][:].indirect(offsets[:, first // 16 : (first + cols) // 16]),
+                                    other,
+                                    MULT,
+                                )
+                                z_bf = rounded.tile([P, cols], BF16, name="z_bf")
+                                nc.scalar.activation(z_bf[:], prod[:], COPY, scale=factor)
+                                for sub in range(cols // BANK):
+                                    bank = first // BANK + sub
+                                    for blk in range(E_BLOCKS):
+                                        nc.tensor.matmul(
+                                            e_ps[blk][bank][:],
+                                            w_sb[:, pair_block, blk * P : (blk + 1) * P],
+                                            z_bf[:, sub * BANK : (sub + 1) * BANK],
+                                            start=(added[bank] == 0),
+                                            stop=(added[bank] == product_tiles - 1),
+                                        )
+                                    added[bank] += 1
+                                tile_in_bank = vg * TOGETHER + ug - ug0
+                                if closing and part > 0 and tile_in_bank < len(mlp_steps):
+                                    mlp_steps[tile_in_bank](part - 1)
+        for step in mlp_steps:
+            step(BANKS - 1)

@@ -15,8 +15,6 @@ N = 2048
 FAN = 6144
 SC = 256
 HID = 128
-U_PER = 8
-V_PER = 16
 PIECE = S
 BANK = 512
 BANKS = N // BANK
@@ -29,19 +27,20 @@ FLOPS = 2 * N * (FAN * SC + SC * HID)
 def tile_edgedecoder_b_kernel(tc, x, x_dst, w0, w1, w2, a1, b1, offs, out):
     nc = tc.nc
     alpha = 1.0 / math.sqrt(FAN)
-    kinds = (
-        (0, 32, 1, w0, alpha),
-        (32, 64, 3, w1, alpha / math.sqrt(3.0)),
-        (224, 32, 5, w2, alpha / math.sqrt(5.0)),
+    families = (
+        (4, 2, ((0, 32, 1, w0, alpha),)),
+        (16, 8, ((32, 64, 3, w1, alpha / math.sqrt(3.0)), (224, 32, 4, w2, alpha / math.sqrt(5.0)))),
+        (4, 2, ((352, 32, 1, w2, alpha / math.sqrt(5.0)),)),
     )
-    product_tiles = sum(
-        comps * (mult // U_PER) * (mult // V_PER) for row0, mult, comps, w, factor in kinds
-    )
+    for own_u, own_v, groups in families:
+        assert sum(comps * (mult // own_u) * (mult // own_v) for row0, mult, comps, w, factor in groups) == P
+    product_tiles = sum(own_u * own_v for own_u, own_v, groups in families)
 
     with (
         tc.tile_pool(name="held", bufs=1) as held,
         tc.tile_pool(name="windows", bufs=4 * TOGETHER) as windows,
-        tc.tile_pool(name="others", bufs=16) as others,
+        tc.tile_pool(name="weights", bufs=3 * TOGETHER) as weights,
+        tc.tile_pool(name="others", bufs=20) as others,
         tc.tile_pool(name="products", bufs=4) as products,
         tc.tile_pool(name="rounded", bufs=4) as rounded,
         tc.tile_pool(name="tail", bufs=2) as tail,
@@ -56,6 +55,14 @@ def tile_edgedecoder_b_kernel(tc, x, x_dst, w0, w1, w2, a1, b1, offs, out):
         nc.scalar.dma_start(b1_sb[:], b1)
         silu_first = held.tile([P, 1], F32, name="silu_first")
         nc.scalar.activation(silu_first[:], b1_sb[:], SILU)
+
+        factors = held.tile([P, len(families)], F32, name="factors")
+        for fam, (own_u, own_v, groups) in enumerate(families):
+            p0 = 0
+            for row0, mult, comps, w, factor in groups:
+                taken = comps * (mult // own_u) * (mult // own_v)
+                nc.vector.memset(factors[p0 : p0 + taken, fam : fam + 1], factor)
+                p0 += taken
 
         e_ps = [
             [psum.tile([P, BANK], F32, name="e_ps%d_%d" % (blk, bank)) for bank in range(BANKS)]
@@ -91,71 +98,92 @@ def tile_edgedecoder_b_kernel(tc, x, x_dst, w0, w1, w2, a1, b1, offs, out):
 
         mlp_steps = (round_e, multiply_by_a1, silu_and_store)
 
+
+        def load_window(win, i, own_u, own_v, groups):
+            p0 = 0
+            for row0, mult, comps, w, factor in groups:
+                u_blocks = comps * (mult // own_u)
+                v_blocks = mult // own_v
+                nc.sync.dma_start(
+                    win[p0 : p0 + u_blocks * v_blocks, :],
+                    x[row0 : row0 + comps * mult, :]
+                    .rearrange("(ub i) s -> ub i s", i=own_u)[:, i : i + 1, :]
+                    .to_broadcast([u_blocks, v_blocks, S]),
+                )
+                p0 += u_blocks * v_blocks
+
+        def load_other(other, k, first, own_u, own_v, groups):
+            p0 = 0
+            for row0, mult, comps, w, factor in groups:
+                u_blocks = mult // own_u
+                v_blocks = mult // own_v
+                for m in range(comps):
+                    base = row0 + mult * m
+                    nc.sync.dma_start(
+                        other[p0 : p0 + u_blocks * v_blocks, :],
+                        x_dst[base : base + mult, first : first + PIECE]
+                        .rearrange("(vb k) n -> k vb n", k=own_v)[k : k + 1, :, :]
+                        .to_broadcast([u_blocks, v_blocks, PIECE]),
+                    )
+                    p0 += u_blocks * v_blocks
+
+        def load_weights(wts, i, own_u, own_v, groups):
+            p0 = 0
+            for row0, mult, comps, w, factor in groups:
+                u_blocks = mult // own_u
+                v_blocks = mult // own_v
+                rows_of_i = (
+                    w.rearrange("(ub r) c -> ub r c", r=own_u * mult)[:, i * mult : (i + 1) * mult, :]
+                    .rearrange("ub (vb k) c -> ub vb (k c)", k=own_v)
+                )
+                for m in range(comps):
+                    nc.sync.dma_start(wts[p0 : p0 + u_blocks * v_blocks, :], rows_of_i)
+                    p0 += u_blocks * v_blocks
+
         added = [0] * BANKS
-        for kind, (row0, mult, comps, w, factor) in enumerate(kinds):
-            u_groups = mult // U_PER
-            v_groups = mult // V_PER
-            w_vu = w.rearrange("(u v) k -> v u k", v=mult)
-            w_sb = held.tile([P, v_groups * u_groups, SC], BF16, name="w_sb%d" % kind)
-            for m in range(comps):
-                base = row0 + mult * m
-                dst = {}
-                for ug0 in range(0, u_groups, TOGETHER):
-                    wins = {}
-                    closing = kind == len(kinds) - 1 and m == comps - 1 and ug0 == u_groups - TOGETHER
-                    cols = BANK if closing else PIECE
-                    for part in range(N // cols):
-                        first = part * cols
-                        piece = first // PIECE
-                        for vg in range(v_groups):
-                            v_lo = V_PER * vg
-                            if ug0 == 0:
-                                dst[vg, piece] = others.tile([P, PIECE], F32, name="other")
-                                nc.sync.dma_start(
-                                    dst[vg, piece][:],
-                                    x_dst[base + v_lo : base + v_lo + V_PER, first : first + PIECE]
-                                    .unsqueeze(1)
-                                    .to_broadcast([V_PER, U_PER, PIECE]),
-                                )
-                            other = dst[vg, piece][:, first - piece * PIECE : first - piece * PIECE + cols]
-                            for ug in range(ug0, ug0 + TOGETHER):
-                                u_lo = U_PER * ug
-                                pair_block = vg * u_groups + ug
-                                if part == 0 and vg == 0:
-                                    wins[ug] = windows.tile([P, S], F32, name="win")
-                                    nc.sync.dma_start(
-                                        wins[ug][:],
-                                        x[base + u_lo : base + u_lo + U_PER, :]
-                                        .unsqueeze(0)
-                                        .to_broadcast([V_PER, U_PER, S]),
+        for fam, (own_u, own_v, groups) in enumerate(families):
+            dst = {}
+            for i0 in range(0, own_u, TOGETHER):
+                wins = {}
+                wts = {}
+                closing = fam == len(families) - 1 and i0 == own_u - TOGETHER
+                cols = BANK if closing else PIECE
+                for part in range(N // cols):
+                    first = part * cols
+                    piece = first // PIECE
+                    for k in range(own_v):
+                        if i0 == 0:
+                            dst[k, piece] = others.tile([P, PIECE], F32, name="other")
+                            load_other(dst[k, piece], k, first, own_u, own_v, groups)
+                        other = dst[k, piece][:, first - piece * PIECE : first - piece * PIECE + cols]
+                        for i in range(i0, i0 + TOGETHER):
+                            if part == 0 and k == 0:
+                                wins[i] = windows.tile([P, S], F32, name="win")
+                                load_window(wins[i], i, own_u, own_v, groups)
+                                wts[i] = weights.tile([P, own_v * SC], BF16, name="wts")
+                                load_weights(wts[i], i, own_u, own_v, groups)
+                            prod = products.tile([P, cols], F32, name="prod")
+                            nc.vector.tensor_tensor(
+                                prod[:],
+                                wins[i][:].indirect(offsets[:, first // 16 : (first + cols) // 16]),
+                                other,
+                                MULT,
+                            )
+                            z_bf = rounded.tile([P, cols], BF16, name="z_bf")
+                            nc.scalar.activation(z_bf[:], prod[:], COPY, scale=factors[:, fam : fam + 1])
+                            for sub in range(cols // BANK):
+                                bank = first // BANK + sub
+                                for blk in range(E_BLOCKS):
+                                    nc.tensor.matmul(
+                                        e_ps[blk][bank][:],
+                                        wts[i][:, k * SC + blk * P : k * SC + (blk + 1) * P],
+                                        z_bf[:, sub * BANK : (sub + 1) * BANK],
+                                        start=(added[bank] == 0),
+                                        stop=(added[bank] == product_tiles - 1),
                                     )
-                                if m == 0 and part == 0:
-                                    nc.sync.dma_start(
-                                        w_sb[:, pair_block, :],
-                                        w_vu[v_lo : v_lo + V_PER, u_lo : u_lo + U_PER, :],
-                                    )
-                                prod = products.tile([P, cols], F32, name="prod")
-                                nc.vector.tensor_tensor(
-                                    prod[:],
-                                    wins[ug][:].indirect(offsets[:, first // 16 : (first + cols) // 16]),
-                                    other,
-                                    MULT,
-                                )
-                                z_bf = rounded.tile([P, cols], BF16, name="z_bf")
-                                nc.scalar.activation(z_bf[:], prod[:], COPY, scale=factor)
-                                for sub in range(cols // BANK):
-                                    bank = first // BANK + sub
-                                    for blk in range(E_BLOCKS):
-                                        nc.tensor.matmul(
-                                            e_ps[blk][bank][:],
-                                            w_sb[:, pair_block, blk * P : (blk + 1) * P],
-                                            z_bf[:, sub * BANK : (sub + 1) * BANK],
-                                            start=(added[bank] == 0),
-                                            stop=(added[bank] == product_tiles - 1),
-                                        )
-                                    added[bank] += 1
-                                tile_in_bank = vg * TOGETHER + ug - ug0
-                                if closing and part > 0 and tile_in_bank < len(mlp_steps):
-                                    mlp_steps[tile_in_bank](part - 1)
+                                added[bank] += 1
+                            tile_in_bank = k * TOGETHER + i - i0
+                            if closing and part > 0 and tile_in_bank < len(mlp_steps):
+                                mlp_steps[tile_in_bank](part - 1)
         for step in mlp_steps:
             step(BANKS - 1)

@@ -102,30 +102,30 @@ def tile_edgedecoder_b_kernel(tc, x, x_dst, w0, w1, w2, a1, b1, offs, out):
         def load_window(win, i, own_u, own_v, groups):
             p0 = 0
             for row0, mult, comps, w, factor in groups:
-                u_blocks = comps * (mult // own_u)
-                v_blocks = mult // own_v
-                nc.sync.dma_start(
-                    win[p0 : p0 + u_blocks * v_blocks, :],
-                    x[row0 : row0 + comps * mult, :]
-                    .rearrange("(ub i) s -> ub i s", i=own_u)[:, i : i + 1, :]
-                    .to_broadcast([u_blocks, v_blocks, S]),
-                )
-                p0 += u_blocks * v_blocks
-
-        def load_other(other, k, first, own_u, own_v, groups):
-            p0 = 0
-            for row0, mult, comps, w, factor in groups:
                 u_blocks = mult // own_u
                 v_blocks = mult // own_v
                 for m in range(comps):
                     base = row0 + mult * m
                     nc.sync.dma_start(
-                        other[p0 : p0 + u_blocks * v_blocks, :],
-                        x_dst[base : base + mult, first : first + PIECE]
-                        .rearrange("(vb k) n -> k vb n", k=own_v)[k : k + 1, :, :]
-                        .to_broadcast([u_blocks, v_blocks, PIECE]),
+                        win[p0 : p0 + v_blocks * u_blocks, :],
+                        x[base : base + mult, :]
+                        .rearrange("(ub i) s -> i ub s", i=own_u)[i : i + 1, :, :]
+                        .to_broadcast([v_blocks, u_blocks, S]),
                     )
-                    p0 += u_blocks * v_blocks
+                    p0 += v_blocks * u_blocks
+
+        def load_other(other, k, first, own_u, own_v, groups):
+            p0 = 0
+            for row0, mult, comps, w, factor in groups:
+                u_blocks = mult // own_u
+                v_blocks = comps * (mult // own_v)
+                nc.sync.dma_start(
+                    other[p0 : p0 + v_blocks * u_blocks, :],
+                    x_dst[row0 : row0 + comps * mult, first : first + PIECE]
+                    .rearrange("(vb k) n -> vb k n", k=own_v)[:, k : k + 1, :]
+                    .to_broadcast([v_blocks, u_blocks, PIECE]),
+                )
+                p0 += v_blocks * u_blocks
 
         def load_weights(wts, i, own_u, own_v, groups):
             p0 = 0
@@ -134,7 +134,7 @@ def tile_edgedecoder_b_kernel(tc, x, x_dst, w0, w1, w2, a1, b1, offs, out):
                 v_blocks = mult // own_v
                 rows_of_i = (
                     w.rearrange("(ub r) c -> ub r c", r=own_u * mult)[:, i * mult : (i + 1) * mult, :]
-                    .rearrange("ub (vb k) c -> ub vb (k c)", k=own_v)
+                    .rearrange("ub (vb k) c -> vb ub (k c)", k=own_v)
                 )
                 for m in range(comps):
                     nc.sync.dma_start(wts[p0 : p0 + u_blocks * v_blocks, :], rows_of_i)

@@ -115,17 +115,18 @@ def tile_edgedecoder_b_kernel(tc, x, x_dst, w0, w1, w2, a1, b1, offs, out):
                     p0 += v_blocks * u_blocks
 
         def load_other(other, k, first, own_u, own_v, groups):
-            p0 = 0
-            for row0, mult, comps, w, factor in groups:
-                u_blocks = mult // own_u
-                v_blocks = comps * (mult // own_v)
-                nc.sync.dma_start(
-                    other[p0 : p0 + v_blocks * u_blocks, :],
-                    x_dst[row0 : row0 + comps * mult, first : first + PIECE]
-                    .rearrange("(vb k) n -> vb k n", k=own_v)[:, k : k + 1, :]
-                    .to_broadcast([v_blocks, u_blocks, PIECE]),
-                )
-                p0 += v_blocks * u_blocks
+            for lo in range(0, PIECE, BANK):
+                p0 = 0
+                for row0, mult, comps, w, factor in groups:
+                    u_blocks = mult // own_u
+                    v_blocks = comps * (mult // own_v)
+                    nc.sync.dma_start(
+                        other[p0 : p0 + v_blocks * u_blocks, lo : lo + BANK],
+                        x_dst[row0 : row0 + comps * mult, first + lo : first + lo + BANK]
+                        .rearrange("(vb k) n -> vb k n", k=own_v)[:, k : k + 1, :]
+                        .to_broadcast([v_blocks, u_blocks, BANK]),
+                    )
+                    p0 += v_blocks * u_blocks
 
         def load_weights(wts, i, own_u, own_v, groups):
             p0 = 0

@@ -19,6 +19,7 @@ PIECE = S
 BANK = 512
 BANKS = N // BANK
 TOGETHER = 2
+RUN = 2048
 E_BLOCKS = SC // P
 
 FLOPS = 2 * N * (FAN * SC + SC * HID)
@@ -100,46 +101,51 @@ def tile_edgedecoder_b_kernel(tc, x, x_dst, w0, w1, w2, a1, b1, offs, out):
 
 
         def load_window(win, i, own_u, own_v, groups):
-            p0 = 0
-            for row0, mult, comps, w, factor in groups:
-                u_blocks = mult // own_u
-                v_blocks = mult // own_v
-                for m in range(comps):
-                    base = row0 + mult * m
-                    nc.sync.dma_start(
-                        win[p0 : p0 + v_blocks * u_blocks, :],
-                        x[base : base + mult, :]
-                        .rearrange("(ub i) s -> i ub s", i=own_u)[i : i + 1, :, :]
-                        .to_broadcast([v_blocks, u_blocks, S]),
-                    )
-                    p0 += v_blocks * u_blocks
+            for lo in range(0, S, RUN // 4):
+                p0 = 0
+                for row0, mult, comps, w, factor in groups:
+                    u_blocks = mult // own_u
+                    v_blocks = mult // own_v
+                    for m in range(comps):
+                        base = row0 + mult * m
+                        nc.sync.dma_start(
+                            win[p0 : p0 + v_blocks * u_blocks, lo : lo + RUN // 4],
+                            x[base : base + mult, lo : lo + RUN // 4]
+                            .rearrange("(ub i) s -> i ub s", i=own_u)[i : i + 1, :, :]
+                            .to_broadcast([v_blocks, u_blocks, RUN // 4]),
+                        )
+                        p0 += v_blocks * u_blocks
 
         def load_other(other, k, first, own_u, own_v, groups):
-            for lo in range(0, PIECE, BANK):
+            for lo in range(0, PIECE, RUN // 4):
                 p0 = 0
                 for row0, mult, comps, w, factor in groups:
                     u_blocks = mult // own_u
                     v_blocks = comps * (mult // own_v)
                     nc.sync.dma_start(
-                        other[p0 : p0 + v_blocks * u_blocks, lo : lo + BANK],
-                        x_dst[row0 : row0 + comps * mult, first + lo : first + lo + BANK]
+                        other[p0 : p0 + v_blocks * u_blocks, lo : lo + RUN // 4],
+                        x_dst[row0 : row0 + comps * mult, first + lo : first + lo + RUN // 4]
                         .rearrange("(vb k) n -> vb k n", k=own_v)[:, k : k + 1, :]
-                        .to_broadcast([v_blocks, u_blocks, BANK]),
+                        .to_broadcast([v_blocks, u_blocks, RUN // 4]),
                     )
                     p0 += v_blocks * u_blocks
 
         def load_weights(wts, i, own_u, own_v, groups):
-            p0 = 0
-            for row0, mult, comps, w, factor in groups:
-                u_blocks = mult // own_u
-                v_blocks = mult // own_v
-                rows_of_i = (
-                    w.rearrange("(ub r) c -> ub r c", r=own_u * mult)[:, i * mult : (i + 1) * mult, :]
-                    .rearrange("ub (vb k) c -> vb ub (k c)", k=own_v)
-                )
-                for m in range(comps):
-                    nc.sync.dma_start(wts[p0 : p0 + u_blocks * v_blocks, :], rows_of_i)
-                    p0 += u_blocks * v_blocks
+            run = min(RUN // 2, own_v * SC)
+            for lo in range(0, own_v * SC, run):
+                p0 = 0
+                for row0, mult, comps, w, factor in groups:
+                    u_blocks = mult // own_u
+                    v_blocks = mult // own_v
+                    rows_of_i = (
+                        w.rearrange("(ub r) c -> ub r c", r=own_u * mult)[:, i * mult : (i + 1) * mult, :]
+                        .rearrange("ub (vb k) c -> vb ub (k c)", k=own_v)
+                    )
+                    for m in range(comps):
+                        nc.sync.dma_start(
+                            wts[p0 : p0 + u_blocks * v_blocks, lo : lo + run], rows_of_i[:, :, lo : lo + run]
+                        )
+                        p0 += u_blocks * v_blocks
 
         added = [0] * BANKS
         for fam, (own_u, own_v, groups) in enumerate(families):

@@ -20,6 +20,7 @@ BANK = 512
 BANKS = N // BANK
 TOGETHER = 2
 RUN = 2048
+LEAST = 32 * 1024
 E_BLOCKS = SC // P
 
 FLOPS = 2 * N * (FAN * SC + SC * HID)
@@ -100,21 +101,25 @@ def tile_edgedecoder_b_kernel(tc, x, x_dst, w0, w1, w2, a1, b1, offs, out):
         mlp_steps = (round_e, multiply_by_a1, silu_and_store)
 
 
+        def run_of(partitions):
+            return max(RUN, LEAST // partitions)
+
         def load_window(win, i, own_u, own_v, groups):
-            for lo in range(0, S, RUN // 4):
-                p0 = 0
-                for row0, mult, comps, w, factor in groups:
-                    u_blocks = mult // own_u
-                    v_blocks = mult // own_v
-                    for m in range(comps):
-                        base = row0 + mult * m
+            p0 = 0
+            for row0, mult, comps, w, factor in groups:
+                u_blocks = mult // own_u
+                v_blocks = mult // own_v
+                cols = run_of(v_blocks * u_blocks) // 4
+                for m in range(comps):
+                    base = row0 + mult * m
+                    for lo in range(0, S, cols):
                         nc.sync.dma_start(
-                            win[p0 : p0 + v_blocks * u_blocks, lo : lo + RUN // 4],
-                            x[base : base + mult, lo : lo + RUN // 4]
+                            win[p0 : p0 + v_blocks * u_blocks, lo : lo + cols],
+                            x[base : base + mult, lo : lo + cols]
                             .rearrange("(ub i) s -> i ub s", i=own_u)[i : i + 1, :, :]
-                            .to_broadcast([v_blocks, u_blocks, RUN // 4]),
+                            .to_broadcast([v_blocks, u_blocks, cols]),
                         )
-                        p0 += v_blocks * u_blocks
+                    p0 += v_blocks * u_blocks
 
         def load_other(other, k, first, own_u, own_v, groups):
             for lo in range(0, PIECE, RUN // 4):
@@ -131,21 +136,21 @@ def tile_edgedecoder_b_kernel(tc, x, x_dst, w0, w1, w2, a1, b1, offs, out):
                     p0 += v_blocks * u_blocks
 
         def load_weights(wts, i, own_u, own_v, groups):
-            run = min(RUN // 2, own_v * SC)
-            for lo in range(0, own_v * SC, run):
-                p0 = 0
-                for row0, mult, comps, w, factor in groups:
-                    u_blocks = mult // own_u
-                    v_blocks = mult // own_v
-                    rows_of_i = (
-                        w.rearrange("(ub r) c -> ub r c", r=own_u * mult)[:, i * mult : (i + 1) * mult, :]
-                        .rearrange("ub (vb k) c -> vb ub (k c)", k=own_v)
-                    )
-                    for m in range(comps):
+            p0 = 0
+            for row0, mult, comps, w, factor in groups:
+                u_blocks = mult // own_u
+                v_blocks = mult // own_v
+                run = min(run_of(u_blocks * v_blocks) // 2, own_v * SC)
+                rows_of_i = (
+                    w.rearrange("(ub r) c -> ub r c", r=own_u * mult)[:, i * mult : (i + 1) * mult, :]
+                    .rearrange("ub (vb k) c -> vb ub (k c)", k=own_v)
+                )
+                for m in range(comps):
+                    for lo in range(0, own_v * SC, run):
                         nc.sync.dma_start(
                             wts[p0 : p0 + u_blocks * v_blocks, lo : lo + run], rows_of_i[:, :, lo : lo + run]
                         )
-                        p0 += u_blocks * v_blocks
+                    p0 += u_blocks * v_blocks
 
         added = [0] * BANKS
         for fam, (own_u, own_v, groups) in enumerate(families):

@@ -21,6 +21,7 @@ BANKS = N // BANK
 TOGETHER = 2
 RUN = 2048
 LEAST = 32 * 1024
+FIRST_RUN = 4096
 E_BLOCKS = SC // P
 
 FLOPS = 2 * N * (FAN * SC + SC * HID)
@@ -101,15 +102,15 @@ def tile_edgedecoder_b_kernel(tc, x, x_dst, w0, w1, w2, a1, b1, offs, out):
         mlp_steps = (round_e, multiply_by_a1, silu_and_store)
 
 
-        def run_of(partitions):
-            return max(RUN, LEAST // partitions)
+        def run_of(run, partitions):
+            return max(run, LEAST // partitions)
 
-        def load_window(win, i, own_u, own_v, groups):
+        def load_window(win, i, run, own_u, own_v, groups):
             p0 = 0
             for row0, mult, comps, w, factor in groups:
                 u_blocks = mult // own_u
                 v_blocks = mult // own_v
-                cols = run_of(v_blocks * u_blocks) // 4
+                cols = run_of(run, v_blocks * u_blocks) // 4
                 for m in range(comps):
                     base = row0 + mult * m
                     for lo in range(0, S, cols):
@@ -121,34 +122,34 @@ def tile_edgedecoder_b_kernel(tc, x, x_dst, w0, w1, w2, a1, b1, offs, out):
                         )
                     p0 += v_blocks * u_blocks
 
-        def load_other(other, k, first, own_u, own_v, groups):
-            for lo in range(0, PIECE, RUN // 4):
+        def load_other(other, k, first, run, own_u, own_v, groups):
+            for lo in range(0, PIECE, run // 4):
                 p0 = 0
                 for row0, mult, comps, w, factor in groups:
                     u_blocks = mult // own_u
                     v_blocks = comps * (mult // own_v)
                     nc.sync.dma_start(
-                        other[p0 : p0 + v_blocks * u_blocks, lo : lo + RUN // 4],
-                        x_dst[row0 : row0 + comps * mult, first + lo : first + lo + RUN // 4]
+                        other[p0 : p0 + v_blocks * u_blocks, lo : lo + run // 4],
+                        x_dst[row0 : row0 + comps * mult, first + lo : first + lo + run // 4]
                         .rearrange("(vb k) n -> vb k n", k=own_v)[:, k : k + 1, :]
-                        .to_broadcast([v_blocks, u_blocks, RUN // 4]),
+                        .to_broadcast([v_blocks, u_blocks, run // 4]),
                     )
                     p0 += v_blocks * u_blocks
 
-        def load_weights(wts, i, own_u, own_v, groups):
+        def load_weights(wts, i, run, own_u, own_v, groups):
             p0 = 0
             for row0, mult, comps, w, factor in groups:
                 u_blocks = mult // own_u
                 v_blocks = mult // own_v
-                run = min(run_of(u_blocks * v_blocks) // 2, own_v * SC)
+                elements = min(run_of(run, u_blocks * v_blocks) // 2, own_v * SC)
                 rows_of_i = (
                     w.rearrange("(ub r) c -> ub r c", r=own_u * mult)[:, i * mult : (i + 1) * mult, :]
                     .rearrange("ub (vb k) c -> vb ub (k c)", k=own_v)
                 )
                 for m in range(comps):
-                    for lo in range(0, own_v * SC, run):
+                    for lo in range(0, own_v * SC, elements):
                         nc.sync.dma_start(
-                            wts[p0 : p0 + u_blocks * v_blocks, lo : lo + run], rows_of_i[:, :, lo : lo + run]
+                            wts[p0 : p0 + u_blocks * v_blocks, lo : lo + elements], rows_of_i[:, :, lo : lo + elements]
                         )
                     p0 += u_blocks * v_blocks
 
@@ -160,20 +161,21 @@ def tile_edgedecoder_b_kernel(tc, x, x_dst, w0, w1, w2, a1, b1, offs, out):
                 wts = {}
                 closing = fam == len(families) - 1 and i0 == own_u - TOGETHER
                 cols = BANK if closing else PIECE
+                run = FIRST_RUN if fam == 0 and i0 == 0 else RUN
                 for part in range(N // cols):
                     first = part * cols
                     piece = first // PIECE
                     for k in range(own_v):
                         if i0 == 0:
                             dst[k, piece] = others.tile([P, PIECE], F32, name="other")
-                            load_other(dst[k, piece], k, first, own_u, own_v, groups)
+                            load_other(dst[k, piece], k, first, run, own_u, own_v, groups)
                         other = dst[k, piece][:, first - piece * PIECE : first - piece * PIECE + cols]
                         for i in range(i0, i0 + TOGETHER):
                             if part == 0 and k == 0:
                                 wins[i] = windows.tile([P, S], F32, name="win")
-                                load_window(wins[i], i, own_u, own_v, groups)
+                                load_window(wins[i], i, run, own_u, own_v, groups)
                                 wts[i] = weights.tile([P, own_v * SC], BF16, name="wts")
-                                load_weights(wts[i], i, own_u, own_v, groups)
+                                load_weights(wts[i], i, run, own_u, own_v, groups)
                             prod = products.tile([P, cols], F32, name="prod")
                             nc.vector.tensor_tensor(
                                 prod[:],

@@ -21,7 +21,7 @@ BANKS = N // BANK
 TOGETHER = 2
 RUN = 2048
 LEAST = 32 * 1024
-FIRST_RUN = 4096
+FIRST_RUN = 1024
 E_BLOCKS = SC // P
 
 FLOPS = 2 * N * (FAN * SC + SC * HID)

@@ -22,6 +22,7 @@ TOGETHER = 2
 RUN = 2048
 LEAST = 32 * 1024
 FIRST_RUN = 1024
+OPENING = (128, 128, 256, 256, 256)
 E_BLOCKS = SC // P
 
 FLOPS = 2 * N * (FAN * SC + SC * HID)
@@ -122,19 +123,21 @@ def tile_edgedecoder_b_kernel(tc, x, x_dst, w0, w1, w2, a1, b1, offs, out):
                         )
                     p0 += v_blocks * u_blocks
 
-        def load_other(other, k, first, run, own_u, own_v, groups):
-            for lo in range(0, PIECE, run // 4):
+        def load_other(other, k, first, widths, own_u, own_v, groups):
+            lo = 0
+            for width in widths:
                 p0 = 0
                 for row0, mult, comps, w, factor in groups:
                     u_blocks = mult // own_u
                     v_blocks = comps * (mult // own_v)
                     nc.sync.dma_start(
-                        other[p0 : p0 + v_blocks * u_blocks, lo : lo + run // 4],
-                        x_dst[row0 : row0 + comps * mult, first + lo : first + lo + run // 4]
+                        other[p0 : p0 + v_blocks * u_blocks, lo : lo + width],
+                        x_dst[row0 : row0 + comps * mult, first + lo : first + lo + width]
                         .rearrange("(vb k) n -> vb k n", k=own_v)[:, k : k + 1, :]
-                        .to_broadcast([v_blocks, u_blocks, run // 4]),
+                        .to_broadcast([v_blocks, u_blocks, width]),
                     )
                     p0 += v_blocks * u_blocks
+                lo += width
 
         def load_weights(wts, i, run, own_u, own_v, groups):
             p0 = 0
@@ -162,27 +165,40 @@ def tile_edgedecoder_b_kernel(tc, x, x_dst, w0, w1, w2, a1, b1, offs, out):
                 closing = fam == len(families) - 1 and i0 == own_u - TOGETHER
                 cols = BANK if closing else PIECE
                 run = FIRST_RUN if fam == 0 and i0 == 0 else RUN
+                even = (run // 4,) * (PIECE * 4 // run)
+                if fam == 0 and i0 == 0:
+                    for i, k in ((0, 0), (1, 1)):
+                        wins[i] = windows.tile([P, S], F32, name="win")
+                        load_window(wins[i], i, run, own_u, own_v, groups)
+                        dst[k, 0] = others.tile([P, PIECE], F32, name="other")
+                        load_other(dst[k, 0], k, 0, OPENING if k == 0 else even, own_u, own_v, groups)
+                    for i in (0, 1):
+                        wts[i] = weights.tile([P, own_v * SC], BF16, name="wts")
+                        load_weights(wts[i], i, run, own_u, own_v, groups)
                 for part in range(N // cols):
                     first = part * cols
                     piece = first // PIECE
                     for k in range(own_v):
-                        if i0 == 0:
+                        if i0 == 0 and (k, piece) not in dst:
                             dst[k, piece] = others.tile([P, PIECE], F32, name="other")
-                            load_other(dst[k, piece], k, first, run, own_u, own_v, groups)
+                            load_other(dst[k, piece], k, first, even, own_u, own_v, groups)
                         other = dst[k, piece][:, first - piece * PIECE : first - piece * PIECE + cols]
                         for i in range(i0, i0 + TOGETHER):
-                            if part == 0 and k == 0:
+                            if part == 0 and k == 0 and i not in wins:
                                 wins[i] = windows.tile([P, S], F32, name="win")
                                 load_window(wins[i], i, run, own_u, own_v, groups)
                                 wts[i] = weights.tile([P, own_v * SC], BF16, name="wts")
                                 load_weights(wts[i], i, run, own_u, own_v, groups)
                             prod = products.tile([P, cols], F32, name="prod")
-                            nc.vector.tensor_tensor(
-                                prod[:],
-                                wins[i][:].indirect(offsets[:, first // 16 : (first + cols) // 16]),
-                                other,
-                                MULT,
-                            )
+                            lo = 0
+                            for width in OPENING if fam == 0 and part == 0 and k == 0 and i == 0 else (cols,):
+                                nc.vector.tensor_tensor(
+                                    prod[:, lo : lo + width],
+                                    wins[i][:].indirect(offsets[:, (first + lo) // 16 : (first + lo + width) // 16]),
+                                    other[:, lo : lo + width],
+                                    MULT,
+                                )
+                                lo += width
                             z_bf = rounded.tile([P, cols], BF16, name="z_bf")
                             nc.scalar.activation(z_bf[:], prod[:], COPY, scale=factors[:, fam : fam + 1])
                             for sub in range(cols // BANK):

@@ -54,11 +54,7 @@ def tile_edgedecoder_b_kernel(tc, x, x_dst, w0, w1, w2, a1, b1, offs, out):
         nc.sync.dma_start(offsets[:], offs)
 
         a1_sb = held.tile([P, E_BLOCKS, HID], BF16, name="a1_sb")
-        nc.scalar.dma_start(a1_sb[:], a1.rearrange("(blk p) r -> p blk r", p=P))
         b1_sb = held.tile([P, 1], F32, name="b1_sb")
-        nc.scalar.dma_start(b1_sb[:], b1)
-        silu_first = held.tile([P, 1], F32, name="silu_first")
-        nc.scalar.activation(silu_first[:], b1_sb[:], SILU)
 
         factors = held.tile([P, len(families)], F32, name="factors")
         for fam, (own_u, own_v, groups) in enumerate(families):
@@ -67,6 +63,8 @@ def tile_edgedecoder_b_kernel(tc, x, x_dst, w0, w1, w2, a1, b1, offs, out):
                 taken = comps * (mult // own_u) * (mult // own_v)
                 nc.vector.memset(factors[p0 : p0 + taken, fam : fam + 1], factor)
                 p0 += taken
+        silu_first = held.tile([P, 1], F32, name="silu_first")
+        nc.scalar.activation(silu_first[:], factors[:, 0:1], SILU)
 
         e_ps = [
             [psum.tile([P, BANK], F32, name="e_ps%d_%d" % (blk, bank)) for bank in range(BANKS)]
@@ -175,6 +173,8 @@ def tile_edgedecoder_b_kernel(tc, x, x_dst, w0, w1, w2, a1, b1, offs, out):
                     for i in (0, 1):
                         wts[i] = weights.tile([P, own_v * SC], BF16, name="wts")
                         load_weights(wts[i], i, run, own_u, own_v, groups)
+                    nc.sync.dma_start(a1_sb[:], a1.rearrange("(blk p) r -> p blk r", p=P))
+                    nc.sync.dma_start(b1_sb[:], b1)
                 for part in range(N // cols):
                     first = part * cols
                     piece = first // PIECE

@@ -24,6 +24,7 @@ LEAST = 32 * 1024
 FIRST_RUN = 1024
 OPENING = (128, 128, 256, 256, 256)
 E_BLOCKS = SC // P
+GAP = 56 * 1024
 
 FLOPS = 2 * N * (FAN * SC + SC * HID)
 
@@ -45,9 +46,9 @@ def tile_edgedecoder_b_kernel(tc, x, x_dst, w0, w1, w2, a1, b1, offs, out):
         tc.tile_pool(name="windows", bufs=4 * TOGETHER) as windows,
         tc.tile_pool(name="weights", bufs=3 * TOGETHER) as weights,
         tc.tile_pool(name="others", bufs=20) as others,
-        tc.tile_pool(name="products", bufs=4) as products,
         tc.tile_pool(name="rounded", bufs=4) as rounded,
         tc.tile_pool(name="tail", bufs=2) as tail,
+        tc.tile_pool(name="products", bufs=4) as products,
         tc.psum_pool(name="psum", bufs=1) as psum,
     ):
         offsets = held.tile([P, N // 16], U16, name="offsets")
@@ -189,7 +190,7 @@ def tile_edgedecoder_b_kernel(tc, x, x_dst, w0, w1, w2, a1, b1, offs, out):
                                 load_window(wins[i], i, run, own_u, own_v, groups)
                                 wts[i] = weights.tile([P, own_v * SC], BF16, name="wts")
                                 load_weights(wts[i], i, run, own_u, own_v, groups)
-                            prod = products.tile([P, cols], F32, name="prod")
+                            prod = products.tile([P, cols], F32, name="prod", offset=GAP)
                             lo = 0
                             for width in OPENING if fam == 0 and part == 0 and k == 0 and i == 0 else (cols,):
                                 nc.vector.tensor_tensor(

import math

import concourse.mybir as mybir

F32 = mybir.dt.float32
BF16 = mybir.dt.bfloat16
U16 = mybir.dt.uint16
MULT = mybir.AluOpType.mult
COPY = mybir.ActivationFunctionType.Copy
SILU = mybir.ActivationFunctionType.Silu

P = 128
S = 1024
N = 2048
FAN = 6144
SC = 256
HID = 128
PIECE = S
BANK = 512
BANKS = N // BANK
TOGETHER = 2
RUN = 2048
LEAST = 32 * 1024
FIRST_RUN = 1024
OPENING = (128, 128, 256, 256, 256)
E_BLOCKS = SC // P
GAP = 56 * 1024

FLOPS = 2 * N * (FAN * SC + SC * HID)


def tile_edgedecoder_b_kernel(tc, x, x_dst, w0, w1, w2, a1, b1, offs, out):
    nc = tc.nc
    alpha = 1.0 / math.sqrt(FAN)
    families = (
        (4, 2, ((0, 32, 1, w0, alpha),)),
        (16, 8, ((32, 64, 3, w1, alpha / math.sqrt(3.0)), (224, 32, 4, w2, alpha / math.sqrt(5.0)))),
        (4, 2, ((352, 32, 1, w2, alpha / math.sqrt(5.0)),)),
    )
    for own_u, own_v, groups in families:
        assert sum(comps * (mult // own_u) * (mult // own_v) for row0, mult, comps, w, factor in groups) == P
    product_tiles = sum(own_u * own_v for own_u, own_v, groups in families)

    with (
        tc.tile_pool(name="held", bufs=1) as held,
        tc.tile_pool(name="windows", bufs=4 * TOGETHER) as windows,
        tc.tile_pool(name="weights", bufs=3 * TOGETHER) as weights,
        tc.tile_pool(name="others", bufs=20) as others,
        tc.tile_pool(name="rounded", bufs=4) as rounded,
        tc.tile_pool(name="tail", bufs=2) as tail,
        tc.tile_pool(name="products", bufs=4) as products,
        tc.psum_pool(name="psum", bufs=1) as psum,
    ):
        offsets = held.tile([P, N // 16], U16, name="offsets")
        nc.sync.dma_start(offsets[:], offs)

        a1_sb = held.tile([P, E_BLOCKS, HID], BF16, name="a1_sb")
        b1_sb = held.tile([P, 1], F32, name="b1_sb")

        factors = held.tile([P, len(families)], F32, name="factors")
        for fam, (own_u, own_v, groups) in enumerate(families):
            p0 = 0
            for row0, mult, comps, w, factor in groups:
                taken = comps * (mult // own_u) * (mult // own_v)
                nc.vector.memset(factors[p0 : p0 + taken, fam : fam + 1], factor)
                p0 += taken
        silu_first = held.tile([P, 1], F32, name="silu_first")
        nc.scalar.activation(silu_first[:], factors[:, 0:1], SILU)

        e_ps = [
            [psum.tile([P, BANK], F32, name="e_ps%d_%d" % (blk, bank)) for bank in range(BANKS)]
            for blk in range(E_BLOCKS)
        ]

        e_bf = {}
        h_ps = {}

        def round_e(bank):
            e_bf[bank] = [tail.tile([P, BANK], BF16, name="e_bf%d" % blk) for blk in range(E_BLOCKS)]
            if bank == BANKS - 1:
                nc.vector.tensor_copy(e_bf[bank][0][:], e_ps[0][bank][:])
            else:
                nc.scalar.copy(e_bf[bank][0][:], e_ps[0][bank][:])
            nc.scalar.copy(e_bf[bank][1][:], e_ps[1][bank][:])

        def multiply_by_a1(bank):
            h_ps[bank] = psum.tile([P, BANK], F32, name="h_ps", tag="e_ps0_%d" % bank)
            for blk in range(E_BLOCKS):
                nc.tensor.matmul(
                    h_ps[bank][:],
                    a1_sb[:, blk, :],
                    e_bf[bank][blk][:],
                    start=(blk == 0),
                    stop=(blk == E_BLOCKS - 1),
                )

        def silu_and_store(bank):
            out_sb = tail.tile([P, BANK], F32, name="out_sb")
            nc.scalar.activation(out_sb[:], h_ps[bank][:], SILU, bias=b1_sb[:, 0:1])
            nc.sync.dma_start(out[:, bank * BANK : (bank + 1) * BANK], out_sb[:])

        mlp_steps = (round_e, multiply_by_a1, silu_and_store)


        def run_of(run, partitions):
            return max(run, LEAST // partitions)

        def load_window(win, i, run, own_u, own_v, groups):
            p0 = 0
            for row0, mult, comps, w, factor in groups:
                u_blocks = mult // own_u
                v_blocks = mult // own_v
                cols = run_of(run, v_blocks * u_blocks) // 4
                for m in range(comps):
                    base = row0 + mult * m
                    for lo in range(0, S, cols):
                        nc.sync.dma_start(
                            win[p0 : p0 + v_blocks * u_blocks, lo : lo + cols],
                            x[base : base + mult, lo : lo + cols]
                            .rearrange("(ub i) s -> i ub s", i=own_u)[i : i + 1, :, :]
                            .to_broadcast([v_blocks, u_blocks, cols]),
                        )
                    p0 += v_blocks * u_blocks

        def load_other(other, k, first, widths, own_u, own_v, groups):
            lo = 0
            for width in widths:
                p0 = 0
                for row0, mult, comps, w, factor in groups:
                    u_blocks = mult // own_u
                    v_blocks = comps * (mult // own_v)
                    nc.sync.dma_start(
                        other[p0 : p0 + v_blocks * u_blocks, lo : lo + width],
                        x_dst[row0 : row0 + comps * mult, first + lo : first + lo + width]
                        .rearrange("(vb k) n -> vb k n", k=own_v)[:, k : k + 1, :]
                        .to_broadcast([v_blocks, u_blocks, width]),
                    )
                    p0 += v_blocks * u_blocks
                lo += width

        def load_weights(wts, i, run, own_u, own_v, groups):
            p0 = 0
            for row0, mult, comps, w, factor in groups:
                u_blocks = mult // own_u
                v_blocks = mult // own_v
                elements = min(run_of(run, u_blocks * v_blocks) // 2, own_v * SC)
                rows_of_i = (
                    w.rearrange("(ub r) c -> ub r c", r=own_u * mult)[:, i * mult : (i + 1) * mult, :]
                    .rearrange("ub (vb k) c -> vb ub (k c)", k=own_v)
                )
                for m in range(comps):
                    for lo in range(0, own_v * SC, elements):
                        nc.sync.dma_start(
                            wts[p0 : p0 + u_blocks * v_blocks, lo : lo + elements], rows_of_i[:, :, lo : lo + elements]
                        )
                    p0 += u_blocks * v_blocks

        added = [0] * BANKS
        for fam, (own_u, own_v, groups) in enumerate(families):
            dst = {}
            for i0 in range(0, own_u, TOGETHER):
                wins = {}
                wts = {}
                closing = fam == len(families) - 1 and i0 == own_u - TOGETHER
                cols = BANK if closing else PIECE
                run = FIRST_RUN if fam == 0 and i0 == 0 else RUN
                even = (run // 4,) * (PIECE * 4 // run)
                if fam == 0 and i0 == 0:
                    for i, k in ((0, 0), (1, 1)):
                        wins[i] = windows.tile([P, S], F32, name="win")
                        load_window(wins[i], i, run, own_u, own_v, groups)
                        dst[k, 0] = others.tile([P, PIECE], F32, name="other")
                        load_other(dst[k, 0], k, 0, OPENING if k == 0 else even, own_u, own_v, groups)
                    for i in (0, 1):
                        wts[i] = weights.tile([P, own_v * SC], BF16, name="wts")
                        load_weights(wts[i], i, run, own_u, own_v, groups)
                    nc.sync.dma_start(a1_sb[:], a1.rearrange("(blk p) r -> p blk r", p=P))
                    nc.sync.dma_start(b1_sb[:], b1)
                for part in range(N // cols):
                    first = part * cols
                    piece = first // PIECE
                    for k in range(own_v):
                        if i0 == 0 and (k, piece) not in dst:
                            dst[k, piece] = others.tile([P, PIECE], F32, name="other")
                            load_other(dst[k, piece], k, first, even, own_u, own_v, groups)
                        other = dst[k, piece][:, first - piece * PIECE : first - piece * PIECE + cols]
                        for i in range(i0, i0 + TOGETHER):
                            if part == 0 and k == 0 and i not in wins:
                                wins[i] = windows.tile([P, S], F32, name="win")
                                load_window(wins[i], i, run, own_u, own_v, groups)
                                wts[i] = weights.tile([P, own_v * SC], BF16, name="wts")
                                load_weights(wts[i], i, run, own_u, own_v, groups)
                            prod = products.tile([P, cols], F32, name="prod", offset=GAP)
                            lo = 0
                            for width in OPENING if fam == 0 and part == 0 and k == 0 and i == 0 else (cols,):
                                nc.vector.tensor_tensor(
                                    prod[:, lo : lo + width],
                                    wins[i][:].indirect(offsets[:, (first + lo) // 16 : (first + lo + width) // 16]),
                                    other[:, lo : lo + width],
                                    MULT,
                                )
                                lo += width
                            z_bf = rounded.tile([P, cols], BF16, name="z_bf")
                            nc.scalar.activation(z_bf[:], prod[:], COPY, scale=factors[:, fam : fam + 1])
                            for sub in range(cols // BANK):
                                bank = first // BANK + sub
                                for blk in range(E_BLOCKS):
                                    nc.tensor.matmul(
                                        e_ps[blk][bank][:],
                                        wts[i][:, k * SC + blk * P : k * SC + (blk + 1) * P],
                                        z_bf[:, sub * BANK : (sub + 1) * BANK],
                                        start=(added[bank] == 0),
                                        stop=(added[bank] == product_tiles - 1),
                                    )
                                added[bank] += 1
                            tile_in_bank = k * TOGETHER + i - i0
                            if closing and part > 0 and tile_in_bank < len(mlp_steps):
                                mlp_steps[tile_in_bank](part - 1)
        for step in mlp_steps:
            step(BANKS - 1)
